import numpy as np
import ml_dtypes


def mxq(x, axis, fmt="e4m3"):
    dtype, down = {"e4m3": (ml_dtypes.float8_e4m3fn, 7), "e5m2": (ml_dtypes.float8_e5m2, 14)}[fmt]
    v = np.moveaxis(np.asarray(x, np.float32).astype(ml_dtypes.bfloat16).astype(np.float64), axis, -1)
    blocks = v.reshape(v.shape[:-1] + (-1, 32))
    amax = np.abs(blocks).max(-1, keepdims=True)
    byte = np.maximum(np.where(amax > 0, np.frexp(amax)[1] - 1 + 127, 0) - down, 1)
    scale = np.exp2(byte - 127.0)
    codes = (blocks / scale).astype(np.float32).astype(dtype).astype(np.float64)
    return np.moveaxis((codes * scale).reshape(v.shape), -1, axis)


WIDE = False


def mx_kscale(k):
    if not WIDE:
        return np.ones(k)
    levels = np.array([20, -20, 10, -10, 0])
    a = np.random.permutation(np.resize(levels, k // 512 * 4)).reshape(k // 512, 4)
    idx = np.arange(k)
    return np.exp2(a[idx // 512, idx % 128 // 32])


BF16 = ml_dtypes.bfloat16


def bf(x):
    return np.asarray(x, np.float32).astype(BF16)


def f64(x):
    return np.asarray(x).astype(np.float64)


N, LMAX, CIN, COUT = 512, 1, 128, 512
NL = LMAX + 1
NM = NL * NL


def setup_inputs():
    u = mx_kscale(COUT)
    x = np.random.standard_normal((N, NM, CIN))
    weights = np.random.standard_normal((NL, CIN, COUT)) / np.sqrt(CIN) / u
    path_weights = 1.0 + 0.3 * np.random.standard_normal(NL)
    g = np.random.standard_normal((N, NM, COUT)) * np.exp2(np.random.randint(-12, 1, (N, NM, 1))) * 16.0 * u
    return {"x": bf(x), "weights": bf(weights), "path_weights": bf(path_weights), "grad_out": bf(g)}


def reference(x, weights, path_weights, grad_out):
    weights, path_weights, g = f64(weights), f64(path_weights), f64(grad_out)
    blocks = []
    for l in range(LMAX + 1):
        start = l * l
        end = start + (2 * l + 1)
        blk = mxq(g[:, start:end, :], 2, "e5m2") @ mxq(weights[l], 1, "e4m3").T
        blocks.append(path_weights[l] * blk)
    return np.concatenate(blocks, axis=1)

@@ -1,0 +1,129 @@
+from contextlib import ExitStack
+
+import concourse.mybir as mybir
+from concourse.masks import make_identity
+
+BF16 = mybir.dt.bfloat16
+F32 = mybir.dt.float32
+I32 = mybir.dt.int32
+U32 = mybir.dt.uint32
+U8 = mybir.dt.uint8
+E5M2_X4 = mybir.dt.float8_e5m2_x4
+E4M3_X4 = mybir.dt.float8_e4m3fn_x4
+COPY = mybir.ActivationFunctionType.Copy
+
+P = 128
+NODES = 512
+ROWS = 4
+DEGREES = 2
+DEGREE_ROWS = ((0, 1), (1, 4))
+C_IN = 128
+C_OUT = 512
+GROUPS = NODES // P
+PACK = 4
+HALVES = 2
+PAIR = 2
+WINDOW = ROWS * C_IN
+W_BLOCKS = 2 * ROWS - 1
+W_BLOCK_OF_DEGREE = (0, ROWS)
+
+FLOPS = 2 * NODES * ROWS * C_OUT * C_IN
+BYTES = 2 * (NODES * ROWS * C_OUT + DEGREES * C_IN * C_OUT + DEGREES) + 4 * NODES * ROWS * C_IN
+
+
+def transpose_pair(nc, banks, identity, rows_bf16, grouped_bf16, copy):
+    words = rows_bf16.bitcast(F32)
+    bank = banks.tile([P, PAIR, HALVES, P], F32)
+    for i in range(PAIR):
+        for u in range(HALVES):
+            nc.tensor.transpose(bank[:, i, u, :], words[:, i, u * P : (u + 1) * P], identity)
+    copy(
+        out=grouped_bf16.bitcast(F32).rearrange("p (i r u) -> p i r u", i=PAIR, u=HALVES),
+        in_=bank[:].rearrange("p i u r -> p i r u"),
+    )
+
+
+def tile_linear_pa_s_kernel(tc, x, weights, path_weights, grad_out, out):
+    nc = tc.nc
+    g_groups = grad_out.rearrange("(p a) m k -> p a m k", a=GROUPS)
+    out_groups = out.rearrange("(p a) m c -> p a m c", a=GROUPS)
+
+    with ExitStack() as ctx:
+        once = ctx.enter_context(tc.tile_pool(name="once", bufs=1))
+        per_group = ctx.enter_context(tc.tile_pool(name="per_group", bufs=GROUPS))
+        banks = ctx.enter_context(tc.psum_pool(name="banks", bufs=4))
+        sums = ctx.enter_context(tc.psum_pool(name="sums", bufs=4))
+
+        w_codes = once.tile([P, W_BLOCKS * C_IN], U32, align_bytes=64)
+        w_scales = once.tile([P, W_BLOCKS * C_IN], U8, align_bytes=64)
+        nc.vector.memset(w_codes[:].bitcast(I32), 0)
+        nc.vector.memset(w_scales[:].bitcast(I32), 0)
+
+        identity = once.tile([P, P], F32)
+        make_identity(nc, identity[:])
+
+        w_rows = once.tile([P, DEGREES, C_OUT], BF16)
+        nc.sync.dma_start(out=w_rows[:], in_=weights.rearrange("l c k -> c l k"))
+        g_rows = []
+        for a in range(GROUPS):
+            g_rows_a = per_group.tile([P, ROWS, C_OUT], BF16)
+            nc.sync.dma_start(out=g_rows_a[:], in_=g_groups[:, a])
+            g_rows.append(g_rows_a)
+
+        pw_bf16 = once.tile([P, DEGREES], BF16)
+        nc.scalar.dma_start(out=pw_bf16[:], in_=path_weights.partition_broadcast(P))
+        pw = once.tile([P, DEGREES], F32)
+        nc.gpsimd.tensor_copy(out=pw[:], in_=pw_bf16[:])
+
+        w_grouped = once.tile([P, DEGREES * C_IN * PACK], BF16, align_bytes=64)
+        transpose_pair(nc, banks, identity[:], w_rows[:], w_grouped[:], nc.vector.tensor_copy)
+        for l in range(DEGREES):
+            block = slice(W_BLOCK_OF_DEGREE[l] * C_IN, (W_BLOCK_OF_DEGREE[l] + 1) * C_IN)
+            nc.vector.quantize_mx(
+                out=w_codes[:, block].bitcast(E4M3_X4),
+                scales=w_scales[:, block],
+                in_=w_grouped[:, l * C_IN * PACK : (l + 1) * C_IN * PACK],
+            )
+
+        def transpose_group(a):
+            grouped = per_group.tile([P, ROWS * P * PACK], BF16, align_bytes=64)
+            half = PAIR * P * PACK
+            transpose_pair(nc, banks, identity[:], g_rows[a][:, 0:PAIR, :], grouped[:, 0:half], nc.vector.tensor_copy)
+            transpose_pair(nc, banks, identity[:], g_rows[a][:, PAIR:ROWS, :], grouped[:, half : 2 * half], nc.scalar.copy)
+            return grouped
+
+        grouped_next = transpose_group(0)
+        for a in range(GROUPS):
+            grouped = grouped_next
+            g_codes = per_group.tile([P, ROWS * P], U32, align_bytes=64)
+            g_scales = per_group.tile([P, ROWS * P], U8, align_bytes=64)
+            nc.vector.quantize_mx(out=g_codes[:].bitcast(E5M2_X4), scales=g_scales[:], in_=grouped[:])
+
+            if a + 1 < GROUPS:
+                grouped_next = transpose_group(a + 1)
+
+            acc = sums.tile([P, ROWS, C_IN], F32)
+            for m in range(ROWS):
+                rows_m = slice(m * P, (m + 1) * P)
+                first = ((ROWS - m) % ROWS) * C_IN
+                window = slice(first, first + WINDOW)
+                nc.tensor.matmul_mx(
+                    out=acc[:].rearrange("p m c -> p (m c)"),
+                    lhsT=g_codes[:, rows_m].bitcast(E5M2_X4),
+                    lhsT_scale=g_scales[:, rows_m],
+                    rhs=w_codes[:, window].bitcast(E4M3_X4),
+                    rhs_scale=w_scales[:, window],
+                    start=(m == 0),
+                    stop=(m == ROWS - 1),
+                )
+
+            result = per_group.tile([P, ROWS, C_IN], F32)
+            for l in range(DEGREES):
+                m_first, m_last = DEGREE_ROWS[l]
+                nc.scalar.activation(
+                    out=result[:, m_first:m_last, :],
+                    in_=acc[:, m_first:m_last, :],
+                    func=COPY,
+                    scale=pw[:, l : l + 1],
+                )
+            nc.sync.dma_start(out=out_groups[:, a], in_=result[:])

@@ -11,21 +11,23 @@ U8 = mybir.dt.uint8
 E5M2_X4 = mybir.dt.float8_e5m2_x4
 E4M3_X4 = mybir.dt.float8_e4m3fn_x4
 COPY = mybir.ActivationFunctionType.Copy
+MULT = mybir.AluOpType.mult
 
 P = 128
 NODES = 512
 ROWS = 4
 DEGREES = 2
-DEGREE_ROWS = ((0, 1), (1, 4))
+DEGREE_OF_ROW = (0, 1, 1, 1)
 C_IN = 128
 C_OUT = 512
 GROUPS = NODES // P
 PACK = 4
 HALVES = 2
 PAIR = 2
-WINDOW = ROWS * C_IN
-W_BLOCKS = 2 * ROWS - 1
-W_BLOCK_OF_DEGREE = (0, ROWS)
+PAIRS = ROWS // PAIR
+WINDOW = 512
+W_BLOCK_OF_DEGREE = (0, 4)
+W_BLOCKS = 8
 
 FLOPS = 2 * NODES * ROWS * C_OUT * C_IN
 BYTES = 2 * (NODES * ROWS * C_OUT + DEGREES * C_IN * C_OUT + DEGREES) + 4 * NODES * ROWS * C_IN
@@ -49,8 +51,10 @@ def tile_linear_pa_s_kernel(tc, x, weights, path_weights, grad_out, out):
     out_groups = out.rearrange("(p a) m c -> p a m c", a=GROUPS)
 
     with ExitStack() as ctx:
+        ctx.enter_context(tc.manual_schedule())
         once = ctx.enter_context(tc.tile_pool(name="once", bufs=1))
         per_group = ctx.enter_context(tc.tile_pool(name="per_group", bufs=GROUPS))
+        per_pair = ctx.enter_context(tc.tile_pool(name="per_pair", bufs=GROUPS * PAIRS))
         banks = ctx.enter_context(tc.psum_pool(name="banks", bufs=4))
         sums = ctx.enter_context(tc.psum_pool(name="sums", bufs=4))
 
@@ -64,14 +68,17 @@ def tile_linear_pa_s_kernel(tc, x, weights, path_weights, grad_out, out):
 
         w_rows = once.tile([P, DEGREES, C_OUT], BF16)
         nc.sync.dma_start(out=w_rows[:], in_=weights.rearrange("l c k -> c l k"))
+        pw_bf16 = once.tile([P, DEGREES], BF16)
         g_rows = []
         for a in range(GROUPS):
             g_rows_a = per_group.tile([P, ROWS, C_OUT], BF16)
-            nc.sync.dma_start(out=g_rows_a[:], in_=g_groups[:, a])
+            for h in range(PAIRS):
+                pair_rows = slice(h * PAIR, (h + 1) * PAIR)
+                nc.sync.dma_start(out=g_rows_a[:, pair_rows, :], in_=g_groups[:, a, pair_rows, :])
             g_rows.append(g_rows_a)
+            if a == 1:
+                nc.sync.dma_start(out=pw_bf16[:], in_=path_weights.partition_broadcast(P))
 
-        pw_bf16 = once.tile([P, DEGREES], BF16)
-        nc.scalar.dma_start(out=pw_bf16[:], in_=path_weights.partition_broadcast(P))
         pw = once.tile([P, DEGREES], F32)
         nc.gpsimd.tensor_copy(out=pw[:], in_=pw_bf16[:])
 
@@ -85,45 +92,51 @@ def tile_linear_pa_s_kernel(tc, x, weights, path_weights, grad_out, out):
                 in_=w_grouped[:, l * C_IN * PACK : (l + 1) * C_IN * PACK],
             )
 
-        def transpose_group(a):
+        def prepare(a):
             grouped = per_group.tile([P, ROWS * P * PACK], BF16, align_bytes=64)
             half = PAIR * P * PACK
             transpose_pair(nc, banks, identity[:], g_rows[a][:, 0:PAIR, :], grouped[:, 0:half], nc.vector.tensor_copy)
             transpose_pair(nc, banks, identity[:], g_rows[a][:, PAIR:ROWS, :], grouped[:, half : 2 * half], nc.scalar.copy)
-            return grouped
-
-        grouped_next = transpose_group(0)
-        for a in range(GROUPS):
-            grouped = grouped_next
             g_codes = per_group.tile([P, ROWS * P], U32, align_bytes=64)
             g_scales = per_group.tile([P, ROWS * P], U8, align_bytes=64)
             nc.vector.quantize_mx(out=g_codes[:].bitcast(E5M2_X4), scales=g_scales[:], in_=grouped[:])
+            return g_codes, g_scales
 
+        def multiply(a, g_codes, g_scales):
+            for h in range(PAIRS):
+                acc = sums.tile([P, WINDOW], F32)
+                for i in range(PAIR):
+                    m = h * PAIR + i
+                    rows_m = slice(m * P, (m + 1) * P)
+                    first = (W_BLOCK_OF_DEGREE[DEGREE_OF_ROW[m]] - i) * C_IN
+                    window = slice(first, first + WINDOW)
+                    nc.tensor.matmul_mx(
+                        out=acc[:],
+                        lhsT=g_codes[:, rows_m].bitcast(E5M2_X4),
+                        lhsT_scale=g_scales[:, rows_m],
+                        rhs=w_codes[:, window].bitcast(E4M3_X4),
+                        rhs_scale=w_scales[:, window],
+                        start=(i == 0),
+                        stop=(i == PAIR - 1),
+                    )
+                result = per_pair.tile([P, PAIR * C_IN], F32)
+                if h == 0:
+                    for i in range(PAIR):
+                        l = DEGREE_OF_ROW[i]
+                        cols = slice(i * C_IN, (i + 1) * C_IN)
+                        nc.scalar.activation(out=result[:, cols], in_=acc[:, cols], func=COPY, scale=pw[:, l : l + 1])
+                else:
+                    nc.vector.tensor_scalar(
+                        out=result[:], in0=acc[:, 0 : PAIR * C_IN], scalar1=pw[:, 1:2], scalar2=None, op0=MULT
+                    )
+                nc.sync.dma_start(
+                    out=out_groups[:, a, h * PAIR : (h + 1) * PAIR, :],
+                    in_=result[:].rearrange("p (i c) -> p i c", i=PAIR),
+                )
+
+        ready = prepare(0)
+        for a in range(GROUPS):
+            codes_and_scales = ready
             if a + 1 < GROUPS:
-                grouped_next = transpose_group(a + 1)
-
-            acc = sums.tile([P, ROWS, C_IN], F32)
-            for m in range(ROWS):
-                rows_m = slice(m * P, (m + 1) * P)
-                first = ((ROWS - m) % ROWS) * C_IN
-                window = slice(first, first + WINDOW)
-                nc.tensor.matmul_mx(
-                    out=acc[:].rearrange("p m c -> p (m c)"),
-                    lhsT=g_codes[:, rows_m].bitcast(E5M2_X4),
-                    lhsT_scale=g_scales[:, rows_m],
-                    rhs=w_codes[:, window].bitcast(E4M3_X4),
-                    rhs_scale=w_scales[:, window],
-                    start=(m == 0),
-                    stop=(m == ROWS - 1),
-                )
-
-            result = per_group.tile([P, ROWS, C_IN], F32)
-            for l in range(DEGREES):
-                m_first, m_last = DEGREE_ROWS[l]
-                nc.scalar.activation(
-                    out=result[:, m_first:m_last, :],
-                    in_=acc[:, m_first:m_last, :],
-                    func=COPY,
-                    scale=pw[:, l : l + 1],
-                )
-            nc.sync.dma_start(out=out_groups[:, a], in_=result[:])
+                ready = prepare(a + 1)
+            multiply(a, codes_and_scales[0], codes_and_scales[1])

@@ -10,7 +10,6 @@ U32 = mybir.dt.uint32
 U8 = mybir.dt.uint8
 E5M2_X4 = mybir.dt.float8_e5m2_x4
 E4M3_X4 = mybir.dt.float8_e4m3fn_x4
-COPY = mybir.ActivationFunctionType.Copy
 MULT = mybir.AluOpType.mult
 
 P = 128
@@ -20,41 +19,44 @@ DEGREES = 2
 DEGREE_OF_ROW = (0, 1, 1, 1)
 C_IN = 128
 C_OUT = 512
-GROUPS = NODES // P
 PACK = 4
 HALVES = 2
 PAIR = 2
-PAIRS = ROWS // PAIR
+PAIRS_OF_NODE = ROWS // PAIR
+NODES_OF_PARTITION = NODES // P
+N_PAIRS = NODES_OF_PARTITION * PAIRS_OF_NODE
 WINDOW = 512
 W_BLOCK_OF_DEGREE = (0, 4)
 W_BLOCKS = 8
+T_RUN = 3
+M_RUN = 2
+PAIRS_BEFORE_PATH_WEIGHTS = 4
 
 FLOPS = 2 * NODES * ROWS * C_OUT * C_IN
 BYTES = 2 * (NODES * ROWS * C_OUT + DEGREES * C_IN * C_OUT + DEGREES) + 4 * NODES * ROWS * C_IN
 
 
-def transpose_pair(nc, banks, identity, rows_bf16, grouped_bf16, copy):
+def transpose_pair(nc, banks, identity, rows_bf16, grouped_bf16):
     words = rows_bf16.bitcast(F32)
     bank = banks.tile([P, PAIR, HALVES, P], F32)
     for i in range(PAIR):
-        for u in range(HALVES):
-            nc.tensor.transpose(bank[:, i, u, :], words[:, i, u * P : (u + 1) * P], identity)
-    copy(
-        out=grouped_bf16.bitcast(F32).rearrange("p (i r u) -> p i r u", i=PAIR, u=HALVES),
-        in_=bank[:].rearrange("p i u r -> p i r u"),
+        for v in range(HALVES):
+            nc.tensor.transpose(bank[:, i, v, :], words[:, i, v * P : (v + 1) * P], identity)
+    nc.scalar.copy(
+        out=grouped_bf16.bitcast(F32).rearrange("p (i r v) -> p i r v", i=PAIR, v=HALVES),
+        in_=bank[:].rearrange("p i v r -> p i r v"),
     )
 
 
 def tile_linear_pa_s_kernel(tc, x, weights, path_weights, grad_out, out):
     nc = tc.nc
-    g_groups = grad_out.rearrange("(p a) m k -> p a m k", a=GROUPS)
-    out_groups = out.rearrange("(p a) m c -> p a m c", a=GROUPS)
+    g_pairs = grad_out.rearrange("(p a) (h i) k -> p (a h) i k", a=NODES_OF_PARTITION, i=PAIR)
+    out_pairs = out.rearrange("(p a) (h i) c -> p (a h) i c", a=NODES_OF_PARTITION, i=PAIR)
 
     with ExitStack() as ctx:
         ctx.enter_context(tc.manual_schedule())
         once = ctx.enter_context(tc.tile_pool(name="once", bufs=1))
-        per_group = ctx.enter_context(tc.tile_pool(name="per_group", bufs=GROUPS))
-        per_pair = ctx.enter_context(tc.tile_pool(name="per_pair", bufs=GROUPS * PAIRS))
+        per_pair = ctx.enter_context(tc.tile_pool(name="per_pair", bufs=N_PAIRS))
         banks = ctx.enter_context(tc.psum_pool(name="banks", bufs=4))
         sums = ctx.enter_context(tc.psum_pool(name="sums", bufs=4))
 
@@ -70,20 +72,18 @@ def tile_linear_pa_s_kernel(tc, x, weights, path_weights, grad_out, out):
         nc.sync.dma_start(out=w_rows[:], in_=weights.rearrange("l c k -> c l k"))
         pw_bf16 = once.tile([P, DEGREES], BF16)
         g_rows = []
-        for a in range(GROUPS):
-            g_rows_a = per_group.tile([P, ROWS, C_OUT], BF16)
-            for h in range(PAIRS):
-                pair_rows = slice(h * PAIR, (h + 1) * PAIR)
-                nc.sync.dma_start(out=g_rows_a[:, pair_rows, :], in_=g_groups[:, a, pair_rows, :])
-            g_rows.append(g_rows_a)
-            if a == 1:
+        for u in range(N_PAIRS):
+            if u == PAIRS_BEFORE_PATH_WEIGHTS:
                 nc.sync.dma_start(out=pw_bf16[:], in_=path_weights.partition_broadcast(P))
+            g_rows_u = per_pair.tile([P, PAIR, C_OUT], BF16)
+            nc.sync.dma_start(out=g_rows_u[:], in_=g_pairs[:, u])
+            g_rows.append(g_rows_u)
 
         pw = once.tile([P, DEGREES], F32)
         nc.gpsimd.tensor_copy(out=pw[:], in_=pw_bf16[:])
 
         w_grouped = once.tile([P, DEGREES * C_IN * PACK], BF16, align_bytes=64)
-        transpose_pair(nc, banks, identity[:], w_rows[:], w_grouped[:], nc.vector.tensor_copy)
+        transpose_pair(nc, banks, identity[:], w_rows[:], w_grouped[:])
         for l in range(DEGREES):
             block = slice(W_BLOCK_OF_DEGREE[l] * C_IN, (W_BLOCK_OF_DEGREE[l] + 1) * C_IN)
             nc.vector.quantize_mx(
@@ -92,51 +92,44 @@ def tile_linear_pa_s_kernel(tc, x, weights, path_weights, grad_out, out):
                 in_=w_grouped[:, l * C_IN * PACK : (l + 1) * C_IN * PACK],
             )
 
-        def prepare(a):
-            grouped = per_group.tile([P, ROWS * P * PACK], BF16, align_bytes=64)
-            half = PAIR * P * PACK
-            transpose_pair(nc, banks, identity[:], g_rows[a][:, 0:PAIR, :], grouped[:, 0:half], nc.vector.tensor_copy)
-            transpose_pair(nc, banks, identity[:], g_rows[a][:, PAIR:ROWS, :], grouped[:, half : 2 * half], nc.scalar.copy)
-            g_codes = per_group.tile([P, ROWS * P], U32, align_bytes=64)
-            g_scales = per_group.tile([P, ROWS * P], U8, align_bytes=64)
+        def prepare(u):
+            grouped = per_pair.tile([P, PAIR * P * PACK], BF16, align_bytes=64)
+            transpose_pair(nc, banks, identity[:], g_rows[u][:], grouped[:])
+            g_codes = per_pair.tile([P, PAIR * P], U32, align_bytes=64)
+            g_scales = per_pair.tile([P, PAIR * P], U8, align_bytes=64)
             nc.vector.quantize_mx(out=g_codes[:].bitcast(E5M2_X4), scales=g_scales[:], in_=grouped[:])
             return g_codes, g_scales
 
-        def multiply(a, g_codes, g_scales):
-            for h in range(PAIRS):
-                acc = sums.tile([P, WINDOW], F32)
-                for i in range(PAIR):
-                    m = h * PAIR + i
-                    rows_m = slice(m * P, (m + 1) * P)
-                    first = (W_BLOCK_OF_DEGREE[DEGREE_OF_ROW[m]] - i) * C_IN
-                    window = slice(first, first + WINDOW)
-                    nc.tensor.matmul_mx(
-                        out=acc[:],
-                        lhsT=g_codes[:, rows_m].bitcast(E5M2_X4),
-                        lhsT_scale=g_scales[:, rows_m],
-                        rhs=w_codes[:, window].bitcast(E4M3_X4),
-                        rhs_scale=w_scales[:, window],
-                        start=(i == 0),
-                        stop=(i == PAIR - 1),
-                    )
-                result = per_pair.tile([P, PAIR * C_IN], F32)
-                if h == 0:
-                    for i in range(PAIR):
-                        l = DEGREE_OF_ROW[i]
-                        cols = slice(i * C_IN, (i + 1) * C_IN)
-                        nc.scalar.activation(out=result[:, cols], in_=acc[:, cols], func=COPY, scale=pw[:, l : l + 1])
-                else:
-                    nc.vector.tensor_scalar(
-                        out=result[:], in0=acc[:, 0 : PAIR * C_IN], scalar1=pw[:, 1:2], scalar2=None, op0=MULT
-                    )
-                nc.sync.dma_start(
-                    out=out_groups[:, a, h * PAIR : (h + 1) * PAIR, :],
-                    in_=result[:].rearrange("p (i c) -> p i c", i=PAIR),
+        def multiply(u, g_codes, g_scales):
+            acc = sums.tile([P, WINDOW], F32)
+            result = per_pair.tile([P, PAIR, C_IN], F32)
+            degrees = [DEGREE_OF_ROW[(u % PAIRS_OF_NODE) * PAIR + i] for i in range(PAIR)]
+            for i in range(PAIR):
+                rows_i = slice(i * P, (i + 1) * P)
+                first = (W_BLOCK_OF_DEGREE[degrees[i]] - i) * C_IN
+                window = slice(first, first + WINDOW)
+                nc.tensor.matmul_mx(
+                    out=acc[:],
+                    lhsT=g_codes[:, rows_i].bitcast(E5M2_X4),
+                    lhsT_scale=g_scales[:, rows_i],
+                    rhs=w_codes[:, window].bitcast(E4M3_X4),
+                    rhs_scale=w_scales[:, window],
+                    start=(i == 0),
+                    stop=(i == PAIR - 1),
                 )
+            for i in range(PAIR):
+                nc.vector.tensor_scalar(
+                    out=result[:, i, :],
+                    in0=acc[:, i * C_IN : (i + 1) * C_IN],
+                    scalar1=pw[:, degrees[i] : degrees[i] + 1],
+                    scalar2=None,
+                    op0=MULT,
+                )
+            nc.sync.dma_start(out=out_pairs[:, u], in_=result[:])
 
-        ready = prepare(0)
-        for a in range(GROUPS):
-            codes_and_scales = ready
-            if a + 1 < GROUPS:
-                ready = prepare(a + 1)
-            multiply(a, codes_and_scales[0], codes_and_scales[1])
+        operands = []
+        for step in range(N_PAIRS // M_RUN):
+            for u in range(step * T_RUN, min((step + 1) * T_RUN, N_PAIRS)):
+                operands.append(prepare(u))
+            for u in range(step * M_RUN, (step + 1) * M_RUN):
+                multiply(u, operands[u][0], operands[u][1])

@@ -10,6 +10,7 @@ U32 = mybir.dt.uint32
 U8 = mybir.dt.uint8
 E5M2_X4 = mybir.dt.float8_e5m2_x4
 E4M3_X4 = mybir.dt.float8_e4m3fn_x4
+COPY = mybir.ActivationFunctionType.Copy
 MULT = mybir.AluOpType.mult
 
 P = 128
@@ -28,9 +29,9 @@ N_PAIRS = NODES_OF_PARTITION * PAIRS_OF_NODE
 WINDOW = 512
 W_BLOCK_OF_DEGREE = (0, 4)
 W_BLOCKS = 8
-T_RUN = 3
+SPREAD_COLS = 32
+T_RUN = 4
 M_RUN = 2
-PAIRS_BEFORE_PATH_WEIGHTS = 4
 
 FLOPS = 2 * NODES * ROWS * C_OUT * C_IN
 BYTES = 2 * (NODES * ROWS * C_OUT + DEGREES * C_IN * C_OUT + DEGREES) + 4 * NODES * ROWS * C_IN
@@ -60,6 +61,18 @@ def tile_linear_pa_s_kernel(tc, x, weights, path_weights, grad_out, out):
         banks = ctx.enter_context(tc.psum_pool(name="banks", bufs=4))
         sums = ctx.enter_context(tc.psum_pool(name="sums", bufs=4))
 
+        pw_row = once.tile([P, SPREAD_COLS], BF16)
+        nc.vector.memset(pw_row[:], 0.0)
+        nc.scalar.dma_start(out=pw_row[0:1, 0:DEGREES], in_=path_weights.unsqueeze(0))
+
+        w_rows = once.tile([P, DEGREES, C_OUT], BF16)
+        nc.sync.dma_start(out=w_rows[:], in_=weights.rearrange("l c k -> c l k"))
+        g_rows = []
+        for u in range(N_PAIRS):
+            g_rows_u = per_pair.tile([P, PAIR, C_OUT], BF16)
+            nc.sync.dma_start(out=g_rows_u[:], in_=g_pairs[:, u])
+            g_rows.append(g_rows_u)
+
         w_codes = once.tile([P, W_BLOCKS * C_IN], U32, align_bytes=64)
         w_scales = once.tile([P, W_BLOCKS * C_IN], U8, align_bytes=64)
         nc.vector.memset(w_codes[:].bitcast(I32), 0)
@@ -67,20 +80,8 @@ def tile_linear_pa_s_kernel(tc, x, weights, path_weights, grad_out, out):
 
         identity = once.tile([P, P], F32)
         make_identity(nc, identity[:])
-
-        w_rows = once.tile([P, DEGREES, C_OUT], BF16)
-        nc.sync.dma_start(out=w_rows[:], in_=weights.rearrange("l c k -> c l k"))
-        pw_bf16 = once.tile([P, DEGREES], BF16)
-        g_rows = []
-        for u in range(N_PAIRS):
-            if u == PAIRS_BEFORE_PATH_WEIGHTS:
-                nc.sync.dma_start(out=pw_bf16[:], in_=path_weights.partition_broadcast(P))
-            g_rows_u = per_pair.tile([P, PAIR, C_OUT], BF16)
-            nc.sync.dma_start(out=g_rows_u[:], in_=g_pairs[:, u])
-            g_rows.append(g_rows_u)
-
-        pw = once.tile([P, DEGREES], F32)
-        nc.gpsimd.tensor_copy(out=pw[:], in_=pw_bf16[:])
+        ones = once.tile([P, P], BF16)
+        nc.gpsimd.memset(ones[:], 1.0)
 
         w_grouped = once.tile([P, DEGREES * C_IN * PACK], BF16, align_bytes=64)
         transpose_pair(nc, banks, identity[:], w_rows[:], w_grouped[:])
@@ -100,9 +101,9 @@ def tile_linear_pa_s_kernel(tc, x, weights, path_weights, grad_out, out):
             nc.vector.quantize_mx(out=g_codes[:].bitcast(E5M2_X4), scales=g_scales[:], in_=grouped[:])
             return g_codes, g_scales
 
-        def multiply(u, g_codes, g_scales):
+        def multiply(u, g_codes, g_scales, pw):
             acc = sums.tile([P, WINDOW], F32)
-            result = per_pair.tile([P, PAIR, C_IN], F32)
+            result = per_pair.tile([P, PAIR * C_IN], F32)
             degrees = [DEGREE_OF_ROW[(u % PAIRS_OF_NODE) * PAIR + i] for i in range(PAIR)]
             for i in range(PAIR):
                 rows_i = slice(i * P, (i + 1) * P)
@@ -117,19 +118,29 @@ def tile_linear_pa_s_kernel(tc, x, weights, path_weights, grad_out, out):
                     start=(i == 0),
                     stop=(i == PAIR - 1),
                 )
-            for i in range(PAIR):
+            if degrees[0] == degrees[1]:
+                l = degrees[0]
                 nc.vector.tensor_scalar(
-                    out=result[:, i, :],
-                    in0=acc[:, i * C_IN : (i + 1) * C_IN],
-                    scalar1=pw[:, degrees[i] : degrees[i] + 1],
-                    scalar2=None,
-                    op0=MULT,
+                    out=result[:], in0=acc[:, 0 : PAIR * C_IN], scalar1=pw[:, l : l + 1], scalar2=None, op0=MULT
                 )
-            nc.sync.dma_start(out=out_pairs[:, u], in_=result[:])
+            else:
+                for i in range(PAIR):
+                    l = degrees[i]
+                    cols = slice(i * C_IN, (i + 1) * C_IN)
+                    nc.scalar.activation(out=result[:, cols], in_=acc[:, cols], func=COPY, scale=pw[:, l : l + 1])
+            nc.sync.dma_start(out=out_pairs[:, u], in_=result[:].rearrange("p (i c) -> p i c", i=PAIR))
 
         operands = []
+        for u in range(T_RUN):
+            operands.append(prepare(u))
+
+        spread = sums.tile([P, WINDOW], F32, tag="acc")
+        nc.tensor.matmul(out=spread[:, 0:SPREAD_COLS], lhsT=ones[:], rhs=pw_row[:], start=True, stop=True)
+        pw = once.tile([P, DEGREES], F32)
+        nc.vector.tensor_copy(out=pw[:], in_=spread[:, 0:DEGREES])
+
         for step in range(N_PAIRS // M_RUN):
-            for u in range(step * T_RUN, min((step + 1) * T_RUN, N_PAIRS)):
-                operands.append(prepare(u))
             for u in range(step * M_RUN, (step + 1) * M_RUN):
-                multiply(u, operands[u][0], operands[u][1])
+                multiply(u, operands[u][0], operands[u][1], pw)
+            for u in range((step + 1) * T_RUN, min((step + 2) * T_RUN, N_PAIRS)):
+                operands.append(prepare(u))

@@ -29,7 +29,7 @@ N_PAIRS = NODES_OF_PARTITION * PAIRS_OF_NODE
 WINDOW = 512
 W_BLOCK_OF_DEGREE = (0, 4)
 W_BLOCKS = 8
-SPREAD_COLS = 32
+PAIRS_BEFORE_PATH_WEIGHTS = 4
 T_RUN = 4
 M_RUN = 2
 
@@ -61,14 +61,13 @@ def tile_linear_pa_s_kernel(tc, x, weights, path_weights, grad_out, out):
         banks = ctx.enter_context(tc.psum_pool(name="banks", bufs=4))
         sums = ctx.enter_context(tc.psum_pool(name="sums", bufs=4))
 
-        pw_row = once.tile([P, SPREAD_COLS], BF16)
-        nc.vector.memset(pw_row[:], 0.0)
-        nc.scalar.dma_start(out=pw_row[0:1, 0:DEGREES], in_=path_weights.unsqueeze(0))
-
         w_rows = once.tile([P, DEGREES, C_OUT], BF16)
         nc.sync.dma_start(out=w_rows[:], in_=weights.rearrange("l c k -> c l k"))
+        pw_bf16 = once.tile([P, DEGREES], BF16)
         g_rows = []
         for u in range(N_PAIRS):
+            if u == PAIRS_BEFORE_PATH_WEIGHTS:
+                nc.sync.dma_start(out=pw_bf16[:], in_=path_weights.partition_broadcast(P))
             g_rows_u = per_pair.tile([P, PAIR, C_OUT], BF16)
             nc.sync.dma_start(out=g_rows_u[:], in_=g_pairs[:, u])
             g_rows.append(g_rows_u)
@@ -80,8 +79,9 @@ def tile_linear_pa_s_kernel(tc, x, weights, path_weights, grad_out, out):
 
         identity = once.tile([P, P], F32)
         make_identity(nc, identity[:])
-        ones = once.tile([P, P], BF16)
-        nc.gpsimd.memset(ones[:], 1.0)
+
+        pw = once.tile([P, DEGREES], F32)
+        nc.gpsimd.tensor_copy(out=pw[:], in_=pw_bf16[:])
 
         w_grouped = once.tile([P, DEGREES * C_IN * PACK], BF16, align_bytes=64)
         transpose_pair(nc, banks, identity[:], w_rows[:], w_grouped[:])
@@ -133,11 +133,6 @@ def tile_linear_pa_s_kernel(tc, x, weights, path_weights, grad_out, out):
         operands = []
         for u in range(T_RUN):
             operands.append(prepare(u))
-
-        spread = sums.tile([P, WINDOW], F32, tag="acc")
-        nc.tensor.matmul(out=spread[:, 0:SPREAD_COLS], lhsT=ones[:], rhs=pw_row[:], start=True, stop=True)
-        pw = once.tile([P, DEGREES], F32)
-        nc.vector.tensor_copy(out=pw[:], in_=spread[:, 0:DEGREES])
 
         for step in range(N_PAIRS // M_RUN):
             for u in range(step * M_RUN, (step + 1) * M_RUN):

@@ -31,6 +31,8 @@ W_BLOCK_OF_DEGREE = (0, 4)
 W_BLOCKS = 8
 PAIRS_BEFORE_PATH_WEIGHTS = 4
 T_RUN = 4
+WARM_COLS = 256
+WARM_PASSES = 3
 M_RUN = 2
 
 FLOPS = 2 * NODES * ROWS * C_OUT * C_IN
@@ -72,6 +74,12 @@ def tile_linear_pa_s_kernel(tc, x, weights, path_weights, grad_out, out):
             nc.sync.dma_start(out=g_rows_u[:], in_=g_pairs[:, u])
             g_rows.append(g_rows_u)
 
+        warm = once.tile([P, WARM_COLS], F32)
+        nc.vector.memset(warm[:], 0.0)
+        warm_acc = sums.tile([P, WINDOW], F32, tag="acc")
+        for w in range(WARM_PASSES):
+            nc.tensor.matmul(warm_acc[:, 0:WARM_COLS], lhsT=warm[:, 0:P], rhs=warm[:], start=True, stop=True)
+
         w_codes = once.tile([P, W_BLOCKS * C_IN], U32, align_bytes=64)
         w_scales = once.tile([P, W_BLOCKS * C_IN], U8, align_bytes=64)
         nc.vector.memset(w_codes[:].bitcast(I32), 0)
@@ -102,7 +110,7 @@ def tile_linear_pa_s_kernel(tc, x, weights, path_weights, grad_out, out):
             return g_codes, g_scales
 
         def multiply(u, g_codes, g_scales, pw):
-            acc = sums.tile([P, WINDOW], F32)
+            acc = sums.tile([P, WINDOW], F32, tag="acc")
             result = per_pair.tile([P, PAIR * C_IN], F32)
             degrees = [DEGREE_OF_ROW[(u % PAIRS_OF_NODE) * PAIR + i] for i in range(PAIR)]
             for i in range(PAIR):

@@ -32,7 +32,8 @@ W_BLOCKS = 8
 PAIRS_BEFORE_PATH_WEIGHTS = 4
 T_RUN = 4
 WARM_COLS = 256
-WARM_PASSES = 3
+WARM_AT_START = 2
+WARM_AFTER_PAIR = 1
 M_RUN = 2
 
 FLOPS = 2 * NODES * ROWS * C_OUT * C_IN
@@ -77,8 +78,12 @@ def tile_linear_pa_s_kernel(tc, x, weights, path_weights, grad_out, out):
         warm = once.tile([P, WARM_COLS], F32)
         nc.vector.memset(warm[:], 0.0)
         warm_acc = sums.tile([P, WINDOW], F32, tag="acc")
-        for w in range(WARM_PASSES):
+
+        def warm_pass():
             nc.tensor.matmul(warm_acc[:, 0:WARM_COLS], lhsT=warm[:, 0:P], rhs=warm[:], start=True, stop=True)
+
+        for w in range(WARM_AT_START):
+            warm_pass()
 
         w_codes = once.tile([P, W_BLOCKS * C_IN], U32, align_bytes=64)
         w_scales = once.tile([P, W_BLOCKS * C_IN], U8, align_bytes=64)
@@ -141,6 +146,8 @@ def tile_linear_pa_s_kernel(tc, x, weights, path_weights, grad_out, out):
         operands = []
         for u in range(T_RUN):
             operands.append(prepare(u))
+            if u == WARM_AFTER_PAIR:
+                warm_pass()
 
         for step in range(N_PAIRS // M_RUN):
             for u in range(step * M_RUN, (step + 1) * M_RUN):

@@ -143,6 +143,30 @@ def tile_linear_pa_s_kernel(tc, x, weights, path_weights, grad_out, out):
                     nc.scalar.activation(out=result[:, cols], in_=acc[:, cols], func=COPY, scale=pw[:, l : l + 1])
             nc.sync.dma_start(out=out_pairs[:, u], in_=result[:].rearrange("p (i c) -> p i c", i=PAIR))
 
+        def multiply_apart(u, g_codes, g_scales, pw):
+            for i in range(PAIR):
+                l = DEGREE_OF_ROW[(u % PAIRS_OF_NODE) * PAIR + i]
+                rows_i = slice(i * P, (i + 1) * P)
+                window = slice(W_BLOCK_OF_DEGREE[l] * C_IN, W_BLOCK_OF_DEGREE[l] * C_IN + WINDOW)
+                acc = sums.tile([P, WINDOW], F32, tag="acc")
+                nc.tensor.matmul_mx(
+                    out=acc[:],
+                    lhsT=g_codes[:, rows_i].bitcast(E5M2_X4),
+                    lhsT_scale=g_scales[:, rows_i],
+                    rhs=w_codes[:, window].bitcast(E4M3_X4),
+                    rhs_scale=w_scales[:, window],
+                    start=True,
+                    stop=True,
+                )
+                half = once.tile([P, C_IN], F32, tag="half%d" % i)
+                if i == 0:
+                    nc.scalar.activation(out=half[:], in_=acc[:, 0:C_IN], func=COPY, scale=pw[:, l : l + 1])
+                else:
+                    nc.vector.tensor_scalar(
+                        out=half[:], in0=acc[:, 0:C_IN], scalar1=pw[:, l : l + 1], scalar2=None, op0=MULT
+                    )
+                nc.sync.dma_start(out=out_pairs[:, u, i], in_=half[:])
+
         operands = []
         for u in range(T_RUN):
             operands.append(prepare(u))
@@ -151,6 +175,9 @@ def tile_linear_pa_s_kernel(tc, x, weights, path_weights, grad_out, out):
 
         for step in range(N_PAIRS // M_RUN):
             for u in range(step * M_RUN, (step + 1) * M_RUN):
-                multiply(u, operands[u][0], operands[u][1], pw)
+                if u == N_PAIRS - 1:
+                    multiply_apart(u, operands[u][0], operands[u][1], pw)
+                else:
+                    multiply(u, operands[u][0], operands[u][1], pw)
             for u in range((step + 1) * T_RUN, min((step + 2) * T_RUN, N_PAIRS)):
                 operands.append(prepare(u))

@@ -31,6 +31,7 @@ W_BLOCK_OF_DEGREE = (0, 4)
 W_BLOCKS = 8
 PAIRS_BEFORE_PATH_WEIGHTS = 4
 T_RUN = 4
+PAIR_ORDER = (1, 3, 5, 7, 0, 2, 4, 6)
 WARM_COLS = 256
 WARM_AT_START = 2
 WARM_AFTER_PAIR = 1
@@ -42,7 +43,7 @@ BYTES = 2 * (NODES * ROWS * C_OUT + DEGREES * C_IN * C_OUT + DEGREES) + 4 * NODE
 
 def transpose_pair(nc, banks, identity, rows_bf16, grouped_bf16):
     words = rows_bf16.bitcast(F32)
-    bank = banks.tile([P, PAIR, HALVES, P], F32)
+    bank = banks.tile([P, PAIR, HALVES, P], F32, tag="bank")
     for i in range(PAIR):
         for v in range(HALVES):
             nc.tensor.transpose(bank[:, i, v, :], words[:, i, v * P : (v + 1) * P], identity)
@@ -64,16 +65,17 @@ def tile_linear_pa_s_kernel(tc, x, weights, path_weights, grad_out, out):
         banks = ctx.enter_context(tc.psum_pool(name="banks", bufs=4))
         sums = ctx.enter_context(tc.psum_pool(name="sums", bufs=4))
 
-        w_rows = once.tile([P, DEGREES, C_OUT], BF16)
-        nc.sync.dma_start(out=w_rows[:], in_=weights.rearrange("l c k -> c l k"))
+        w_rows = [once.tile([P, C_OUT], BF16, name="w_rows%d" % l) for l in range(DEGREES)]
+        nc.sync.dma_start(out=w_rows[1][:], in_=weights[1])
         pw_bf16 = once.tile([P, DEGREES], BF16)
-        g_rows = []
-        for u in range(N_PAIRS):
-            if u == PAIRS_BEFORE_PATH_WEIGHTS:
+        g_rows = {}
+        for n, u in enumerate(PAIR_ORDER):
+            if n == PAIRS_BEFORE_PATH_WEIGHTS:
                 nc.sync.dma_start(out=pw_bf16[:], in_=path_weights.partition_broadcast(P))
+                nc.sync.dma_start(out=w_rows[0][:], in_=weights[0])
             g_rows_u = per_pair.tile([P, PAIR, C_OUT], BF16)
             nc.sync.dma_start(out=g_rows_u[:], in_=g_pairs[:, u])
-            g_rows.append(g_rows_u)
+            g_rows[u] = g_rows_u
 
         warm = once.tile([P, WARM_COLS], F32)
         nc.vector.memset(warm[:], 0.0)
@@ -96,23 +98,34 @@ def tile_linear_pa_s_kernel(tc, x, weights, path_weights, grad_out, out):
         pw = once.tile([P, DEGREES], F32)
         nc.gpsimd.tensor_copy(out=pw[:], in_=pw_bf16[:])
 
-        w_grouped = once.tile([P, DEGREES * C_IN * PACK], BF16, align_bytes=64)
-        transpose_pair(nc, banks, identity[:], w_rows[:], w_grouped[:])
-        for l in range(DEGREES):
-            block = slice(W_BLOCK_OF_DEGREE[l] * C_IN, (W_BLOCK_OF_DEGREE[l] + 1) * C_IN)
-            nc.vector.quantize_mx(
-                out=w_codes[:, block].bitcast(E4M3_X4),
-                scales=w_scales[:, block],
-                in_=w_grouped[:, l * C_IN * PACK : (l + 1) * C_IN * PACK],
+        def prepare_weights(l):
+            words = w_rows[l][:].bitcast(F32)
+            bank = banks.tile([P, PAIR, HALVES, P], F32, tag="bank")
+            for v in range(HALVES):
+                nc.tensor.transpose(bank[:, 0, v, :], words[:, v * P : (v + 1) * P], identity[:])
+            w_grouped = once.tile([P, C_IN * PACK], BF16, align_bytes=64, name="w_grouped%d" % l)
+            nc.scalar.copy(
+                out=w_grouped[:].bitcast(F32).rearrange("p (r v) -> p r v", v=HALVES),
+                in_=bank[:, 0].rearrange("p v r -> p r v"),
             )
+            block = slice(W_BLOCK_OF_DEGREE[l] * C_IN, (W_BLOCK_OF_DEGREE[l] + 1) * C_IN)
+            nc.vector.quantize_mx(out=w_codes[:, block].bitcast(E4M3_X4), scales=w_scales[:, block], in_=w_grouped[:])
 
-        def prepare(u):
+        prepare_weights(1)
+
+        def turn(u):
             grouped = per_pair.tile([P, PAIR * P * PACK], BF16, align_bytes=64)
             transpose_pair(nc, banks, identity[:], g_rows[u][:], grouped[:])
+            return grouped
+
+        def quantise(grouped):
             g_codes = per_pair.tile([P, PAIR * P], U32, align_bytes=64)
             g_scales = per_pair.tile([P, PAIR * P], U8, align_bytes=64)
             nc.vector.quantize_mx(out=g_codes[:].bitcast(E5M2_X4), scales=g_scales[:], in_=grouped[:])
             return g_codes, g_scales
+
+        def prepare(u):
+            return quantise(turn(u))
 
         def multiply(u, g_codes, g_scales, pw):
             acc = sums.tile([P, WINDOW], F32, tag="acc")
@@ -167,17 +180,24 @@ def tile_linear_pa_s_kernel(tc, x, weights, path_weights, grad_out, out):
                     )
                 nc.sync.dma_start(out=out_pairs[:, u, i], in_=half[:])
 
-        operands = []
-        for u in range(T_RUN):
-            operands.append(prepare(u))
-            if u == WARM_AFTER_PAIR:
+        operands = {}
+        for n, u in enumerate(PAIR_ORDER[0:T_RUN]):
+            operands[u] = prepare(u)
+            if n == WARM_AFTER_PAIR:
                 warm_pass()
-
-        for step in range(N_PAIRS // M_RUN):
-            for u in range(step * M_RUN, (step + 1) * M_RUN):
-                if u == N_PAIRS - 1:
-                    multiply_apart(u, operands[u][0], operands[u][1], pw)
-                else:
-                    multiply(u, operands[u][0], operands[u][1], pw)
-            for u in range((step + 1) * T_RUN, min((step + 2) * T_RUN, N_PAIRS)):
-                operands.append(prepare(u))
+        for u in PAIR_ORDER[0:M_RUN]:
+            multiply(u, operands[u][0], operands[u][1], pw)
+        prepare_weights(0)
+        turned = {}
+        for u in PAIR_ORDER[T_RUN:N_PAIRS]:
+            turned[u] = turn(u)
+        for n in range(T_RUN, N_PAIRS):
+            u = PAIR_ORDER[n]
+            operands[u] = quantise(turned[u])
+            if n - T_RUN >= 1 and n - T_RUN + 1 < T_RUN:
+                w = PAIR_ORDER[n - T_RUN + 1]
+                multiply(w, operands[w][0], operands[w][1], pw)
+        for u in PAIR_ORDER[T_RUN : N_PAIRS - 1]:
+            multiply(u, operands[u][0], operands[u][1], pw)
+        u = PAIR_ORDER[N_PAIRS - 1]
+        multiply_apart(u, operands[u][0], operands[u][1], pw)

@@ -35,7 +35,7 @@ PAIR_ORDER = (1, 3, 5, 7, 0, 2, 4, 6)
 WARM_COLS = 256
 WARM_AT_START = 2
 WARM_AFTER_PAIR = 1
-M_RUN = 2
+M_RUN = 3
 
 FLOPS = 2 * NODES * ROWS * C_OUT * C_IN
 BYTES = 2 * (NODES * ROWS * C_OUT + DEGREES * C_IN * C_OUT + DEGREES) + 4 * NODES * ROWS * C_IN
@@ -194,8 +194,8 @@ def tile_linear_pa_s_kernel(tc, x, weights, path_weights, grad_out, out):
         for n in range(T_RUN, N_PAIRS):
             u = PAIR_ORDER[n]
             operands[u] = quantise(turned[u])
-            if n - T_RUN >= 1 and n - T_RUN + 1 < T_RUN:
-                w = PAIR_ORDER[n - T_RUN + 1]
+            if n - T_RUN >= 1 and n - T_RUN - 1 + M_RUN < T_RUN:
+                w = PAIR_ORDER[n - T_RUN - 1 + M_RUN]
                 multiply(w, operands[w][0], operands[w][1], pw)
         for u in PAIR_ORDER[T_RUN : N_PAIRS - 1]:
             multiply(u, operands[u][0], operands[u][1], pw)

@@ -74,7 +74,11 @@ def tile_linear_pa_s_kernel(tc, x, weights, path_weights, grad_out, out):
                 nc.sync.dma_start(out=pw_bf16[:], in_=path_weights.partition_broadcast(P))
                 nc.sync.dma_start(out=w_rows[0][:], in_=weights[0])
             g_rows_u = per_pair.tile([P, PAIR, C_OUT], BF16)
-            nc.sync.dma_start(out=g_rows_u[:], in_=g_pairs[:, u])
+            if n == T_RUN - 1:
+                for i in range(PAIR):
+                    nc.sync.dma_start(out=g_rows_u[:, i], in_=g_pairs[:, u, i])
+            else:
+                nc.sync.dma_start(out=g_rows_u[:], in_=g_pairs[:, u])
             g_rows[u] = g_rows_u
 
         warm = once.tile([P, WARM_COLS], F32)

@@ -29,28 +29,10 @@ N_PAIRS = NODES_OF_PARTITION * PAIRS_OF_NODE
 WINDOW = 512
 W_BLOCK_OF_DEGREE = (0, 4)
 W_BLOCKS = 8
-PAIRS_BEFORE_PATH_WEIGHTS = 4
-T_RUN = 4
-PAIR_ORDER = (1, 3, 5, 7, 0, 2, 4, 6)
-WARM_COLS = 256
-WARM_AT_START = 2
-WARM_AFTER_PAIR = 1
-M_RUN = 3
+SWAPPED = (5, 7)
 
 FLOPS = 2 * NODES * ROWS * C_OUT * C_IN
 BYTES = 2 * (NODES * ROWS * C_OUT + DEGREES * C_IN * C_OUT + DEGREES) + 4 * NODES * ROWS * C_IN
-
-
-def transpose_pair(nc, banks, identity, rows_bf16, grouped_bf16):
-    words = rows_bf16.bitcast(F32)
-    bank = banks.tile([P, PAIR, HALVES, P], F32, tag="bank")
-    for i in range(PAIR):
-        for v in range(HALVES):
-            nc.tensor.transpose(bank[:, i, v, :], words[:, i, v * P : (v + 1) * P], identity)
-    nc.scalar.copy(
-        out=grouped_bf16.bitcast(F32).rearrange("p (i r v) -> p i r v", i=PAIR, v=HALVES),
-        in_=bank[:].rearrange("p i v r -> p i r v"),
-    )
 
 
 def tile_linear_pa_s_kernel(tc, x, weights, path_weights, grad_out, out):
@@ -61,35 +43,48 @@ def tile_linear_pa_s_kernel(tc, x, weights, path_weights, grad_out, out):
     with ExitStack() as ctx:
         ctx.enter_context(tc.manual_schedule())
         once = ctx.enter_context(tc.tile_pool(name="once", bufs=1))
-        per_pair = ctx.enter_context(tc.tile_pool(name="per_pair", bufs=N_PAIRS))
         banks = ctx.enter_context(tc.psum_pool(name="banks", bufs=4))
         sums = ctx.enter_context(tc.psum_pool(name="sums", bufs=4))
+        both = tuple(range(PAIR))
 
         w_rows = [once.tile([P, C_OUT], BF16, name="w_rows%d" % l) for l in range(DEGREES)]
-        nc.sync.dma_start(out=w_rows[1][:], in_=weights[1])
         pw_bf16 = once.tile([P, DEGREES], BF16)
-        g_rows = {}
-        for n, u in enumerate(PAIR_ORDER):
-            if n == PAIRS_BEFORE_PATH_WEIGHTS:
-                nc.sync.dma_start(out=pw_bf16[:], in_=path_weights.partition_broadcast(P))
-                nc.sync.dma_start(out=w_rows[0][:], in_=weights[0])
-            g_rows_u = per_pair.tile([P, PAIR, C_OUT], BF16)
-            if n == T_RUN - 1:
-                for i in range(PAIR):
-                    nc.sync.dma_start(out=g_rows_u[:, i], in_=g_pairs[:, u, i])
-            else:
-                nc.sync.dma_start(out=g_rows_u[:], in_=g_pairs[:, u])
-            g_rows[u] = g_rows_u
+        g_rows = [once.tile([P, PAIR, C_OUT], BF16, name="g_rows%d" % u) for u in range(N_PAIRS)]
+        grouped = [once.tile([P, PAIR, P * PACK], BF16, align_bytes=64, name="grouped%d" % u) for u in range(N_PAIRS)]
+        g_codes = [once.tile([P, PAIR * P], U32, align_bytes=64, name="g_codes%d" % u) for u in range(N_PAIRS)]
+        g_scales = [once.tile([P, PAIR * P], U8, align_bytes=64, name="g_scales%d" % u) for u in range(N_PAIRS)]
+        results = [once.tile([P, PAIR, C_IN], F32, name="result%d" % u) for u in range(N_PAIRS)]
+        w_grouped = [once.tile([P, C_IN * PACK], BF16, align_bytes=64, name="w_grouped%d" % l) for l in range(DEGREES)]
 
-        warm = once.tile([P, WARM_COLS], F32)
+        def load_weights(l):
+            nc.sync.dma_start(out=w_rows[l][:], in_=weights[l])
+
+        def load_pair(u):
+            nc.sync.dma_start(out=g_rows[u][:], in_=g_pairs[:, u])
+
+        def load_row(u, i):
+            nc.sync.dma_start(out=g_rows[u][:, i], in_=g_pairs[:, u, i])
+
+        load_weights(1)
+        load_pair(1)
+        load_pair(3)
+        load_pair(5)
+        load_row(7, 0)
+        load_row(7, 1)
+        load_weights(0)
+        nc.sync.dma_start(out=pw_bf16[:], in_=path_weights.partition_broadcast(P))
+        for u in (0, 2, 4, 6):
+            load_pair(u)
+
+        warm = once.tile([P, 256], F32)
         nc.vector.memset(warm[:], 0.0)
         warm_acc = sums.tile([P, WINDOW], F32, tag="acc")
 
-        def warm_pass():
-            nc.tensor.matmul(warm_acc[:, 0:WARM_COLS], lhsT=warm[:, 0:P], rhs=warm[:], start=True, stop=True)
+        def warm_pass(cols):
+            nc.tensor.matmul(warm_acc[:, 0:cols], lhsT=warm[:, 0:P], rhs=warm[:, 0:cols], start=True, stop=True)
 
-        for w in range(WARM_AT_START):
-            warm_pass()
+        warm_pass(256)
+        warm_pass(256)
 
         w_codes = once.tile([P, W_BLOCKS * C_IN], U32, align_bytes=64)
         w_scales = once.tile([P, W_BLOCKS * C_IN], U8, align_bytes=64)
@@ -102,106 +97,193 @@ def tile_linear_pa_s_kernel(tc, x, weights, path_weights, grad_out, out):
         pw = once.tile([P, DEGREES], F32)
         nc.gpsimd.tensor_copy(out=pw[:], in_=pw_bf16[:])
 
-        def prepare_weights(l):
+        w_bank = {}
+        g_bank = {}
+
+        def copy(engine, out, in_):
+            if engine == "scalar":
+                nc.scalar.copy(out=out, in_=in_)
+            else:
+                nc.vector.tensor_copy(out=out, in_=in_)
+
+        def turn_weights(l):
             words = w_rows[l][:].bitcast(F32)
             bank = banks.tile([P, PAIR, HALVES, P], F32, tag="bank")
             for v in range(HALVES):
                 nc.tensor.transpose(bank[:, 0, v, :], words[:, v * P : (v + 1) * P], identity[:])
-            w_grouped = once.tile([P, C_IN * PACK], BF16, align_bytes=64, name="w_grouped%d" % l)
-            nc.scalar.copy(
-                out=w_grouped[:].bitcast(F32).rearrange("p (r v) -> p r v", v=HALVES),
-                in_=bank[:, 0].rearrange("p v r -> p r v"),
+            w_bank[l] = bank
+
+        def group_weights(l, engine):
+            copy(
+                engine,
+                w_grouped[l][:].bitcast(F32).rearrange("p (r v) -> p r v", v=HALVES),
+                w_bank[l][:, 0].rearrange("p v r -> p r v"),
             )
+
+        def quantise_weights(l):
             block = slice(W_BLOCK_OF_DEGREE[l] * C_IN, (W_BLOCK_OF_DEGREE[l] + 1) * C_IN)
-            nc.vector.quantize_mx(out=w_codes[:, block].bitcast(E4M3_X4), scales=w_scales[:, block], in_=w_grouped[:])
+            nc.vector.quantize_mx(out=w_codes[:, block].bitcast(E4M3_X4), scales=w_scales[:, block], in_=w_grouped[l][:])
 
-        prepare_weights(1)
+        def turn(u, rows):
+            bank = banks.tile([P, PAIR, HALVES, P], F32, tag="bank")
+            for i in rows:
+                words = g_rows[u][:, i].bitcast(F32)
+                for v in range(HALVES):
+                    nc.tensor.transpose(bank[:, i, v, :], words[:, v * P : (v + 1) * P], identity[:])
+                g_bank[u, i] = bank
 
-        def turn(u):
-            grouped = per_pair.tile([P, PAIR * P * PACK], BF16, align_bytes=64)
-            transpose_pair(nc, banks, identity[:], g_rows[u][:], grouped[:])
-            return grouped
+        def group(u, rows, engine):
+            span = slice(rows[0], rows[-1] + 1)
+            copy(
+                engine,
+                grouped[u][:, span].rearrange("p i c -> p (i c)").bitcast(F32).rearrange("p (i r v) -> p i r v", i=len(rows), v=HALVES),
+                g_bank[u, rows[0]][:, span].rearrange("p i v r -> p i r v"),
+            )
 
-        def quantise(grouped):
-            g_codes = per_pair.tile([P, PAIR * P], U32, align_bytes=64)
-            g_scales = per_pair.tile([P, PAIR * P], U8, align_bytes=64)
-            nc.vector.quantize_mx(out=g_codes[:].bitcast(E5M2_X4), scales=g_scales[:], in_=grouped[:])
-            return g_codes, g_scales
+        def quantise(u, rows):
+            cols = slice(rows[0] * P, (rows[-1] + 1) * P)
+            nc.vector.quantize_mx(
+                out=g_codes[u][:, cols].bitcast(E5M2_X4),
+                scales=g_scales[u][:, cols],
+                in_=grouped[u][:, rows[0] : rows[-1] + 1].rearrange("p i c -> p (i c)"),
+            )
 
-        def prepare(u):
-            return quantise(turn(u))
+        def degree(u, i):
+            return DEGREE_OF_ROW[(u % PAIRS_OF_NODE) * PAIR + i]
 
-        def multiply(u, g_codes, g_scales, pw):
+        def one_pass(acc, u, i, block, start, stop):
+            rows_i = slice(i * P, (i + 1) * P)
+            first = (W_BLOCK_OF_DEGREE[degree(u, i)] - block) * C_IN
+            window = slice(first, first + WINDOW)
+            nc.tensor.matmul_mx(
+                out=acc[:],
+                lhsT=g_codes[u][:, rows_i].bitcast(E5M2_X4),
+                lhsT_scale=g_scales[u][:, rows_i],
+                rhs=w_codes[:, window].bitcast(E4M3_X4),
+                rhs_scale=w_scales[:, window],
+                start=start,
+                stop=stop,
+            )
+
+        pair_acc = {}
+
+        def multiply(u):
             acc = sums.tile([P, WINDOW], F32, tag="acc")
-            result = per_pair.tile([P, PAIR * C_IN], F32)
-            degrees = [DEGREE_OF_ROW[(u % PAIRS_OF_NODE) * PAIR + i] for i in range(PAIR)]
-            for i in range(PAIR):
-                rows_i = slice(i * P, (i + 1) * P)
-                first = (W_BLOCK_OF_DEGREE[degrees[i]] - i) * C_IN
-                window = slice(first, first + WINDOW)
-                nc.tensor.matmul_mx(
-                    out=acc[:],
-                    lhsT=g_codes[:, rows_i].bitcast(E5M2_X4),
-                    lhsT_scale=g_scales[:, rows_i],
-                    rhs=w_codes[:, window].bitcast(E4M3_X4),
-                    rhs_scale=w_scales[:, window],
-                    start=(i == 0),
-                    stop=(i == PAIR - 1),
-                )
-            if degrees[0] == degrees[1]:
-                l = degrees[0]
-                nc.vector.tensor_scalar(
-                    out=result[:], in0=acc[:, 0 : PAIR * C_IN], scalar1=pw[:, l : l + 1], scalar2=None, op0=MULT
-                )
+            for i in both:
+                one_pass(acc, u, i, i, i == 0, i == PAIR - 1)
+            pair_acc[u] = acc
+
+        def scale(engine, out, in_, l):
+            if engine == "scalar":
+                nc.scalar.activation(out=out, in_=in_, func=COPY, scale=pw[:, l : l + 1])
             else:
-                for i in range(PAIR):
-                    l = degrees[i]
-                    cols = slice(i * C_IN, (i + 1) * C_IN)
-                    nc.scalar.activation(out=result[:, cols], in_=acc[:, cols], func=COPY, scale=pw[:, l : l + 1])
-            nc.sync.dma_start(out=out_pairs[:, u], in_=result[:].rearrange("p (i c) -> p i c", i=PAIR))
+                nc.vector.tensor_scalar(out=out, in0=in_, scalar1=pw[:, l : l + 1], scalar2=None, op0=MULT)
 
-        def multiply_apart(u, g_codes, g_scales, pw):
-            for i in range(PAIR):
-                l = DEGREE_OF_ROW[(u % PAIRS_OF_NODE) * PAIR + i]
-                rows_i = slice(i * P, (i + 1) * P)
-                window = slice(W_BLOCK_OF_DEGREE[l] * C_IN, W_BLOCK_OF_DEGREE[l] * C_IN + WINDOW)
-                acc = sums.tile([P, WINDOW], F32, tag="acc")
-                nc.tensor.matmul_mx(
-                    out=acc[:],
-                    lhsT=g_codes[:, rows_i].bitcast(E5M2_X4),
-                    lhsT_scale=g_scales[:, rows_i],
-                    rhs=w_codes[:, window].bitcast(E4M3_X4),
-                    rhs_scale=w_scales[:, window],
-                    start=True,
-                    stop=True,
-                )
-                half = once.tile([P, C_IN], F32, tag="half%d" % i)
-                if i == 0:
-                    nc.scalar.activation(out=half[:], in_=acc[:, 0:C_IN], func=COPY, scale=pw[:, l : l + 1])
-                else:
-                    nc.vector.tensor_scalar(
-                        out=half[:], in0=acc[:, 0:C_IN], scalar1=pw[:, l : l + 1], scalar2=None, op0=MULT
-                    )
-                nc.sync.dma_start(out=out_pairs[:, u, i], in_=half[:])
+        def finish(u, engine):
+            acc = pair_acc[u]
+            if degree(u, 0) == degree(u, 1):
+                scale(engine, results[u][:].rearrange("p i c -> p (i c)"), acc[:, 0 : PAIR * C_IN], degree(u, 0))
+            else:
+                for i in both:
+                    scale(engine, results[u][:, i], acc[:, i * C_IN : (i + 1) * C_IN], degree(u, i))
+            nc.sync.dma_start(out=out_pairs[:, u], in_=results[u][:])
 
-        operands = {}
-        for n, u in enumerate(PAIR_ORDER[0:T_RUN]):
-            operands[u] = prepare(u)
-            if n == WARM_AFTER_PAIR:
-                warm_pass()
-        for u in PAIR_ORDER[0:M_RUN]:
-            multiply(u, operands[u][0], operands[u][1], pw)
-        prepare_weights(0)
-        turned = {}
-        for u in PAIR_ORDER[T_RUN:N_PAIRS]:
-            turned[u] = turn(u)
-        for n in range(T_RUN, N_PAIRS):
-            u = PAIR_ORDER[n]
-            operands[u] = quantise(turned[u])
-            if n - T_RUN >= 1 and n - T_RUN - 1 + M_RUN < T_RUN:
-                w = PAIR_ORDER[n - T_RUN - 1 + M_RUN]
-                multiply(w, operands[w][0], operands[w][1], pw)
-        for u in PAIR_ORDER[T_RUN : N_PAIRS - 1]:
-            multiply(u, operands[u][0], operands[u][1], pw)
-        u = PAIR_ORDER[N_PAIRS - 1]
-        multiply_apart(u, operands[u][0], operands[u][1], pw)
+        def multiply_and_finish_row(u, i, engine):
+            acc = sums.tile([P, WINDOW], F32, tag="acc")
+            one_pass(acc, u, i, 0, True, True)
+            half = once.tile([P, C_IN], F32, tag="half%d" % i)
+            scale(engine, half[:], acc[:, 0:C_IN], degree(u, i))
+            nc.sync.dma_start(out=out_pairs[:, u, i], in_=half[:])
+
+        swap_codes = once.tile([P, WINDOW], U32, align_bytes=64)
+        swap_scales = once.tile([P, WINDOW], U8, align_bytes=64)
+        swap_sums = once.tile([P, WINDOW], F32)
+        swap_result = once.tile([P, len(SWAPPED), PAIR, C_IN], F32)
+        swap = {}
+
+        def quantise_swapped(u, rows):
+            first = SWAPPED.index(u) * PAIR
+            cols = slice((first + rows[0]) * P, (first + rows[-1] + 1) * P)
+            nc.vector.quantize_mx(
+                out=swap_codes[:, cols].bitcast(E5M2_X4),
+                scales=swap_scales[:, cols],
+                in_=grouped[u][:, rows[0] : rows[-1] + 1].rearrange("p i c -> p (i c)"),
+            )
+
+        def multiply_swapped():
+            acc = sums.tile([P, WINDOW], F32, tag="acc")
+            block = slice(W_BLOCK_OF_DEGREE[1] * C_IN, (W_BLOCK_OF_DEGREE[1] + 1) * C_IN)
+            nc.tensor.matmul_mx(
+                out=acc[:],
+                lhsT=w_codes[:, block].bitcast(E4M3_X4),
+                lhsT_scale=w_scales[:, block],
+                rhs=swap_codes[:].bitcast(E5M2_X4),
+                rhs_scale=swap_scales[:],
+                start=True,
+                stop=True,
+            )
+            swap["acc"] = acc
+
+        def turn_back():
+            bank = banks.tile([P, PAIR, HALVES, P], F32, tag="bank")
+            flat = bank[:].rearrange("p i v r -> p (i v r)")
+            for j in range(len(SWAPPED) * PAIR):
+                cols = slice(j * P, (j + 1) * P)
+                nc.tensor.transpose(flat[:, cols], swap_sums[:, cols], identity[:])
+            swap["bank"] = flat
+
+        def finish_swapped(engine):
+            copy(engine, swap_result[:].rearrange("p u i c -> p (u i c)"), swap["bank"])
+            nc.sync.dma_start(out=out_pairs[:, SWAPPED[0] : SWAPPED[-1] + 1 : 2], in_=swap_result[:])
+
+        turn_weights(1)
+        group_weights(1, "vector")
+        quantise_weights(1)
+        turn(1, both)
+        group(1, both, "vector")
+        warm_pass(128)
+        turn(3, both)
+        group(3, both, "scalar")
+        warm_pass(128)
+        quantise(1, both)
+        quantise(3, both)
+        turn(5, both)
+        group(5, both, "scalar")
+        turn(7, (0,))
+        group(7, (0,), "vector")
+        turn(7, (1,))
+        group(7, (1,), "scalar")
+        turn_weights(0)
+        quantise_swapped(5, both)
+        quantise_swapped(7, (0,))
+        quantise_swapped(7, (1,))
+        group_weights(0, "vector")
+        multiply(1)
+        finish(1, "scalar")
+        multiply(3)
+        multiply_swapped()
+        quantise_weights(0)
+        finish(3, "vector")
+        scale("scalar", swap_sums[:], swap["acc"][:], 1)
+        turn(0, both)
+        group(0, both, "vector")
+        turn(2, both)
+        group(2, both, "scalar")
+        turn(4, both)
+        group(4, both, "scalar")
+        turn(6, both)
+        turn_back()
+        group(6, both, "scalar")
+        quantise(0, both)
+        quantise(2, both)
+        quantise(4, both)
+        quantise(6, both)
+        multiply(0)
+        finish(0, "scalar")
+        finish_swapped("scalar")
+        multiply(2)
+        finish(2, "vector")
+        multiply(4)
+        finish(4, "scalar")
+        multiply_and_finish_row(6, 0, "vector")
+        multiply_and_finish_row(6, 1, "scalar")

@@ -83,8 +83,8 @@ def tile_linear_pa_s_kernel(tc, x, weights, path_weights, grad_out, out):
         def warm_pass(cols):
             nc.tensor.matmul(warm_acc[:, 0:cols], lhsT=warm[:, 0:P], rhs=warm[:, 0:cols], start=True, stop=True)
 
-        warm_pass(256)
-        warm_pass(256)
+        for w in range(2):
+            warm_pass(256)
 
         w_codes = once.tile([P, W_BLOCKS * C_IN], U32, align_bytes=64)
         w_scales = once.tile([P, W_BLOCKS * C_IN], U8, align_bytes=64)
@@ -232,15 +232,16 @@ def tile_linear_pa_s_kernel(tc, x, weights, path_weights, grad_out, out):
                 nc.tensor.transpose(flat[:, cols], swap_sums[:, cols], identity[:])
             swap["bank"] = flat
 
-        def finish_swapped(engine):
-            copy(engine, swap_result[:].rearrange("p u i c -> p (u i c)"), swap["bank"])
-            nc.sync.dma_start(out=out_pairs[:, SWAPPED[0] : SWAPPED[-1] + 1 : 2], in_=swap_result[:])
+        def finish_swapped(n, engine):
+            cols = slice(n * PAIR * C_IN, (n + 1) * PAIR * C_IN)
+            copy(engine, swap_result[:, n].rearrange("p i c -> p (i c)"), swap["bank"][:, cols])
+            nc.sync.dma_start(out=out_pairs[:, SWAPPED[n]], in_=swap_result[:, n])
 
         turn_weights(1)
         group_weights(1, "vector")
         quantise_weights(1)
         turn(1, both)
-        group(1, both, "vector")
+        group(1, both, "scalar")
         warm_pass(128)
         turn(3, both)
         group(3, both, "scalar")
@@ -255,15 +256,14 @@ def tile_linear_pa_s_kernel(tc, x, weights, path_weights, grad_out, out):
         group(7, (1,), "scalar")
         turn_weights(0)
         quantise_swapped(5, both)
-        quantise_swapped(7, (0,))
-        quantise_swapped(7, (1,))
-        group_weights(0, "vector")
+        quantise_swapped(7, both)
         multiply(1)
         finish(1, "scalar")
+        group_weights(0, "scalar")
         multiply(3)
         multiply_swapped()
         quantise_weights(0)
-        finish(3, "vector")
+        finish(3, "scalar")
         scale("scalar", swap_sums[:], swap["acc"][:], 1)
         turn(0, both)
         group(0, both, "vector")
@@ -271,16 +271,17 @@ def tile_linear_pa_s_kernel(tc, x, weights, path_weights, grad_out, out):
         group(2, both, "scalar")
         turn(4, both)
         group(4, both, "scalar")
-        turn(6, both)
         turn_back()
+        turn(6, both)
         group(6, both, "scalar")
         quantise(0, both)
         quantise(2, both)
+        finish_swapped(0, "vector")
         quantise(4, both)
         quantise(6, both)
+        finish_swapped(1, "scalar")
         multiply(0)
         finish(0, "scalar")
-        finish_swapped("scalar")
         multiply(2)
         finish(2, "vector")
         multiply(4)

@@ -49,6 +49,7 @@ def tile_linear_pa_s_kernel(tc, x, weights, path_weights, grad_out, out):
 
         w_rows = [once.tile([P, C_OUT], BF16, name="w_rows%d" % l) for l in range(DEGREES)]
         pw_bf16 = once.tile([P, DEGREES], BF16)
+        nc.gpsimd.memset(pw_bf16[:], 0.0)
         g_rows = [once.tile([P, PAIR, C_OUT], BF16, name="g_rows%d" % u) for u in range(N_PAIRS)]
         grouped = [once.tile([P, PAIR, P * PACK], BF16, align_bytes=64, name="grouped%d" % u) for u in range(N_PAIRS)]
         g_codes = [once.tile([P, PAIR * P], U32, align_bytes=64, name="g_codes%d" % u) for u in range(N_PAIRS)]
@@ -68,11 +69,11 @@ def tile_linear_pa_s_kernel(tc, x, weights, path_weights, grad_out, out):
         load_weights(1)
         load_pair(1)
         load_pair(3)
+        nc.sync.dma_start(out=pw_bf16[0:1, :], in_=path_weights.rearrange("(o l) -> o l", o=1))
         load_pair(5)
         load_row(7, 0)
         load_row(7, 1)
         load_weights(0)
-        nc.sync.dma_start(out=pw_bf16[:], in_=path_weights.partition_broadcast(P))
         for u in (0, 2, 4, 6):
             load_pair(u)
 
@@ -94,8 +95,13 @@ def tile_linear_pa_s_kernel(tc, x, weights, path_weights, grad_out, out):
         identity = once.tile([P, P], F32)
         make_identity(nc, identity[:])
 
+        ones = once.tile([P, P], BF16)
+        nc.gpsimd.memset(ones[:], 1.0)
         pw = once.tile([P, DEGREES], F32)
-        nc.gpsimd.tensor_copy(out=pw[:], in_=pw_bf16[:])
+
+        def spread_path_weights():
+            nc.tensor.matmul(warm_acc[:, 0:DEGREES], lhsT=ones[:], rhs=pw_bf16[:], start=True, stop=True)
+            nc.vector.tensor_copy(out=pw[:], in_=warm_acc[:, 0:DEGREES])
 
         w_bank = {}
         g_bank = {}
@@ -247,6 +253,7 @@ def tile_linear_pa_s_kernel(tc, x, weights, path_weights, grad_out, out):
         group(3, both, "scalar")
         warm_pass(128)
         quantise(1, both)
+        spread_path_weights()
         quantise(3, both)
         turn(5, both)
         group(5, both, "scalar")

from contextlib import ExitStack

import concourse.mybir as mybir
from concourse.masks import make_identity

BF16 = mybir.dt.bfloat16
F32 = mybir.dt.float32
I32 = mybir.dt.int32
U32 = mybir.dt.uint32
U8 = mybir.dt.uint8
E5M2_X4 = mybir.dt.float8_e5m2_x4
E4M3_X4 = mybir.dt.float8_e4m3fn_x4
COPY = mybir.ActivationFunctionType.Copy
MULT = mybir.AluOpType.mult

P = 128
NODES = 512
ROWS = 4
DEGREES = 2
DEGREE_OF_ROW = (0, 1, 1, 1)
C_IN = 128
C_OUT = 512
PACK = 4
HALVES = 2
PAIR = 2
PAIRS_OF_NODE = ROWS // PAIR
NODES_OF_PARTITION = NODES // P
N_PAIRS = NODES_OF_PARTITION * PAIRS_OF_NODE
WINDOW = 512
W_BLOCK_OF_DEGREE = (0, 4)
W_BLOCKS = 8
SWAPPED = (5, 7)

FLOPS = 2 * NODES * ROWS * C_OUT * C_IN
BYTES = 2 * (NODES * ROWS * C_OUT + DEGREES * C_IN * C_OUT + DEGREES) + 4 * NODES * ROWS * C_IN


def tile_linear_pa_s_kernel(tc, x, weights, path_weights, grad_out, out):
    nc = tc.nc
    g_pairs = grad_out.rearrange("(p a) (h i) k -> p (a h) i k", a=NODES_OF_PARTITION, i=PAIR)
    out_pairs = out.rearrange("(p a) (h i) c -> p (a h) i c", a=NODES_OF_PARTITION, i=PAIR)

    with ExitStack() as ctx:
        ctx.enter_context(tc.manual_schedule())
        once = ctx.enter_context(tc.tile_pool(name="once", bufs=1))
        banks = ctx.enter_context(tc.psum_pool(name="banks", bufs=4))
        sums = ctx.enter_context(tc.psum_pool(name="sums", bufs=4))
        both = tuple(range(PAIR))

        w_rows = [once.tile([P, C_OUT], BF16, name="w_rows%d" % l) for l in range(DEGREES)]
        pw_bf16 = once.tile([P, DEGREES], BF16)
        nc.gpsimd.memset(pw_bf16[:], 0.0)
        g_rows = [once.tile([P, PAIR, C_OUT], BF16, name="g_rows%d" % u) for u in range(N_PAIRS)]
        grouped = [once.tile([P, PAIR, P * PACK], BF16, align_bytes=64, name="grouped%d" % u) for u in range(N_PAIRS)]
        g_codes = [once.tile([P, PAIR * P], U32, align_bytes=64, name="g_codes%d" % u) for u in range(N_PAIRS)]
        g_scales = [once.tile([P, PAIR * P], U8, align_bytes=64, name="g_scales%d" % u) for u in range(N_PAIRS)]
        results = [once.tile([P, PAIR, C_IN], F32, name="result%d" % u) for u in range(N_PAIRS)]
        w_grouped = [once.tile([P, C_IN * PACK], BF16, align_bytes=64, name="w_grouped%d" % l) for l in range(DEGREES)]

        def load_weights(l):
            nc.sync.dma_start(out=w_rows[l][:], in_=weights[l])

        def load_pair(u):
            nc.sync.dma_start(out=g_rows[u][:], in_=g_pairs[:, u])

        def load_row(u, i):
            nc.sync.dma_start(out=g_rows[u][:, i], in_=g_pairs[:, u, i])

        load_weights(1)
        load_pair(1)
        load_pair(3)
        nc.sync.dma_start(out=pw_bf16[0:1, :], in_=path_weights.rearrange("(o l) -> o l", o=1))
        load_pair(5)
        load_row(7, 0)
        load_row(7, 1)
        load_weights(0)
        for u in (0, 2, 4, 6):
            load_pair(u)

        warm = once.tile([P, 256], F32)
        nc.vector.memset(warm[:], 0.0)
        warm_acc = sums.tile([P, WINDOW], F32, tag="acc")

        def warm_pass(cols):
            nc.tensor.matmul(warm_acc[:, 0:cols], lhsT=warm[:, 0:P], rhs=warm[:, 0:cols], start=True, stop=True)

        for w in range(2):
            warm_pass(256)

        w_codes = once.tile([P, W_BLOCKS * C_IN], U32, align_bytes=64)
        w_scales = once.tile([P, W_BLOCKS * C_IN], U8, align_bytes=64)
        nc.vector.memset(w_codes[:].bitcast(I32), 0)
        nc.vector.memset(w_scales[:].bitcast(I32), 0)

        identity = once.tile([P, P], F32)
        make_identity(nc, identity[:])

        ones = once.tile([P, P], BF16)
        nc.gpsimd.memset(ones[:], 1.0)
        pw = once.tile([P, DEGREES], F32)

        def spread_path_weights():
            nc.tensor.matmul(warm_acc[:, 0:DEGREES], lhsT=ones[:], rhs=pw_bf16[:], start=True, stop=True)
            nc.vector.tensor_copy(out=pw[:], in_=warm_acc[:, 0:DEGREES])

        w_bank = {}
        g_bank = {}

        def copy(engine, out, in_):
            if engine == "scalar":
                nc.scalar.copy(out=out, in_=in_)
            else:
                nc.vector.tensor_copy(out=out, in_=in_)

        def turn_weights(l):
            words = w_rows[l][:].bitcast(F32)
            bank = banks.tile([P, PAIR, HALVES, P], F32, tag="bank")
            for v in range(HALVES):
                nc.tensor.transpose(bank[:, 0, v, :], words[:, v * P : (v + 1) * P], identity[:])
            w_bank[l] = bank

        def group_weights(l, engine):
            copy(
                engine,
                w_grouped[l][:].bitcast(F32).rearrange("p (r v) -> p r v", v=HALVES),
                w_bank[l][:, 0].rearrange("p v r -> p r v"),
            )

        def quantise_weights(l):
            block = slice(W_BLOCK_OF_DEGREE[l] * C_IN, (W_BLOCK_OF_DEGREE[l] + 1) * C_IN)
            nc.vector.quantize_mx(out=w_codes[:, block].bitcast(E4M3_X4), scales=w_scales[:, block], in_=w_grouped[l][:])

        def turn(u, rows):
            bank = banks.tile([P, PAIR, HALVES, P], F32, tag="bank")
            for i in rows:
                words = g_rows[u][:, i].bitcast(F32)
                for v in range(HALVES):
                    nc.tensor.transpose(bank[:, i, v, :], words[:, v * P : (v + 1) * P], identity[:])
                g_bank[u, i] = bank

        def group(u, rows, engine):
            span = slice(rows[0], rows[-1] + 1)
            copy(
                engine,
                grouped[u][:, span].rearrange("p i c -> p (i c)").bitcast(F32).rearrange("p (i r v) -> p i r v", i=len(rows), v=HALVES),
                g_bank[u, rows[0]][:, span].rearrange("p i v r -> p i r v"),
            )

        def quantise(u, rows):
            cols = slice(rows[0] * P, (rows[-1] + 1) * P)
            nc.vector.quantize_mx(
                out=g_codes[u][:, cols].bitcast(E5M2_X4),
                scales=g_scales[u][:, cols],
                in_=grouped[u][:, rows[0] : rows[-1] + 1].rearrange("p i c -> p (i c)"),
            )

        def degree(u, i):
            return DEGREE_OF_ROW[(u % PAIRS_OF_NODE) * PAIR + i]

        def one_pass(acc, u, i, block, start, stop):
            rows_i = slice(i * P, (i + 1) * P)
            first = (W_BLOCK_OF_DEGREE[degree(u, i)] - block) * C_IN
            window = slice(first, first + WINDOW)
            nc.tensor.matmul_mx(
                out=acc[:],
                lhsT=g_codes[u][:, rows_i].bitcast(E5M2_X4),
                lhsT_scale=g_scales[u][:, rows_i],
                rhs=w_codes[:, window].bitcast(E4M3_X4),
                rhs_scale=w_scales[:, window],
                start=start,
                stop=stop,
            )

        pair_acc = {}

        def multiply(u):
            acc = sums.tile([P, WINDOW], F32, tag="acc")
            for i in both:
                one_pass(acc, u, i, i, i == 0, i == PAIR - 1)
            pair_acc[u] = acc

        def scale(engine, out, in_, l):
            if engine == "scalar":
                nc.scalar.activation(out=out, in_=in_, func=COPY, scale=pw[:, l : l + 1])
            else:
                nc.vector.tensor_scalar(out=out, in0=in_, scalar1=pw[:, l : l + 1], scalar2=None, op0=MULT)

        def finish(u, engine):
            acc = pair_acc[u]
            if degree(u, 0) == degree(u, 1):
                scale(engine, results[u][:].rearrange("p i c -> p (i c)"), acc[:, 0 : PAIR * C_IN], degree(u, 0))
            else:
                for i in both:
                    scale(engine, results[u][:, i], acc[:, i * C_IN : (i + 1) * C_IN], degree(u, i))
            nc.sync.dma_start(out=out_pairs[:, u], in_=results[u][:])

        def multiply_and_finish_row(u, i, engine):
            acc = sums.tile([P, WINDOW], F32, tag="acc")
            one_pass(acc, u, i, 0, True, True)
            half = once.tile([P, C_IN], F32, tag="half%d" % i)
            scale(engine, half[:], acc[:, 0:C_IN], degree(u, i))
            nc.sync.dma_start(out=out_pairs[:, u, i], in_=half[:])

        swap_codes = once.tile([P, WINDOW], U32, align_bytes=64)
        swap_scales = once.tile([P, WINDOW], U8, align_bytes=64)
        swap_sums = once.tile([P, WINDOW], F32)
        swap_result = once.tile([P, len(SWAPPED), PAIR, C_IN], F32)
        swap = {}

        def quantise_swapped(u, rows):
            first = SWAPPED.index(u) * PAIR
            cols = slice((first + rows[0]) * P, (first + rows[-1] + 1) * P)
            nc.vector.quantize_mx(
                out=swap_codes[:, cols].bitcast(E5M2_X4),
                scales=swap_scales[:, cols],
                in_=grouped[u][:, rows[0] : rows[-1] + 1].rearrange("p i c -> p (i c)"),
            )

        def multiply_swapped():
            acc = sums.tile([P, WINDOW], F32, tag="acc")
            block = slice(W_BLOCK_OF_DEGREE[1] * C_IN, (W_BLOCK_OF_DEGREE[1] + 1) * C_IN)
            nc.tensor.matmul_mx(
                out=acc[:],
                lhsT=w_codes[:, block].bitcast(E4M3_X4),
                lhsT_scale=w_scales[:, block],
                rhs=swap_codes[:].bitcast(E5M2_X4),
                rhs_scale=swap_scales[:],
                start=True,
                stop=True,
            )
            swap["acc"] = acc

        def turn_back():
            bank = banks.tile([P, PAIR, HALVES, P], F32, tag="bank")
            flat = bank[:].rearrange("p i v r -> p (i v r)")
            for j in range(len(SWAPPED) * PAIR):
                cols = slice(j * P, (j + 1) * P)
                nc.tensor.transpose(flat[:, cols], swap_sums[:, cols], identity[:])
            swap["bank"] = flat

        def finish_swapped(n, engine):
            cols = slice(n * PAIR * C_IN, (n + 1) * PAIR * C_IN)
            copy(engine, swap_result[:, n].rearrange("p i c -> p (i c)"), swap["bank"][:, cols])
            nc.sync.dma_start(out=out_pairs[:, SWAPPED[n]], in_=swap_result[:, n])

        turn_weights(1)
        group_weights(1, "vector")
        quantise_weights(1)
        turn(1, both)
        group(1, both, "scalar")
        warm_pass(128)
        turn(3, both)
        group(3, both, "scalar")
        warm_pass(128)
        quantise(1, both)
        spread_path_weights()
        quantise(3, both)
        turn(5, both)
        group(5, both, "scalar")
        turn(7, (0,))
        group(7, (0,), "vector")
        turn(7, (1,))
        group(7, (1,), "scalar")
        turn_weights(0)
        quantise_swapped(5, both)
        quantise_swapped(7, both)
        multiply(1)
        finish(1, "scalar")
        group_weights(0, "scalar")
        multiply(3)
        multiply_swapped()
        quantise_weights(0)
        finish(3, "scalar")
        scale("scalar", swap_sums[:], swap["acc"][:], 1)
        turn(0, both)
        group(0, both, "vector")
        turn(2, both)
        group(2, both, "scalar")
        turn(4, both)
        group(4, both, "scalar")
        turn_back()
        turn(6, both)
        group(6, both, "scalar")
        quantise(0, both)
        quantise(2, both)
        finish_swapped(0, "vector")
        quantise(4, both)
        quantise(6, both)
        finish_swapped(1, "scalar")
        multiply(0)
        finish(0, "scalar")
        multiply(2)
        finish(2, "vector")
        multiply(4)
        finish(4, "scalar")
        multiply_and_finish_row(6, 0, "vector")
        multiply_and_finish_row(6, 1, "scalar")
